import numpy as np
import ml_dtypes


def mxq(x, axis, fmt="e4m3"):
    dtype, down = {"e4m3": (ml_dtypes.float8_e4m3fn, 7), "e5m2": (ml_dtypes.float8_e5m2, 14)}[fmt]
    v = np.moveaxis(np.asarray(x, np.float32).astype(ml_dtypes.bfloat16).astype(np.float64), axis, -1)
    blocks = v.reshape(v.shape[:-1] + (-1, 32))
    amax = np.abs(blocks).max(-1, keepdims=True)
    byte = np.maximum(np.where(amax > 0, np.frexp(amax)[1] - 1 + 127, 0) - down, 1)
    scale = np.exp2(byte - 127.0)
    codes = (blocks / scale).astype(np.float32).astype(dtype).astype(np.float64)
    return np.moveaxis((codes * scale).reshape(v.shape), -1, axis)


WIDE = False


def mx_kscale(k):
    if not WIDE:
        return np.ones(k)
    levels = np.array([10, -10, 5, -5, 0])
    a = np.random.permutation(np.resize(levels, k // 512 * 4)).reshape(k // 512, 4)
    idx = np.arange(k)
    return np.exp2(a[idx // 512, idx % 128 // 32])


BF16 = ml_dtypes.bfloat16


def bf(x):
    return np.asarray(x, np.float32).astype(BF16)


def f64(x):
    return np.asarray(x).astype(np.float64)


L, N, E, H, C, LW, RW = 2048, 1, 1024, 8, 512, 1, 1
EPS = 1e-8


def sigmoid(v):
    return 1.0 / (1.0 + np.exp(-v))


def setup_inputs():
    s = mx_kscale(E)
    return {"attn_out": bf(np.random.standard_normal((L, N, E)) * 2.0),
            "norm_scale": bf((1.0 + 0.1 * np.random.standard_normal(E)) * s),
            "norm_gate": bf(1.0 + 0.2 * np.random.standard_normal(E)),
            "w_o": bf(np.random.standard_normal((E, E)) / np.sqrt(E) / s[None, :]),
            "b_o": bf(np.random.standard_normal(E) * 0.1)}


def reference(attn_out, norm_scale, norm_gate, w_o, b_o):
    x = f64(attn_out)
    rms = np.sqrt(np.mean(x * x, axis=-1, keepdims=True))
    y = f64(norm_scale) * (x / (rms + EPS)) * sigmoid(f64(norm_gate) * x)
    return (mxq(y, 2, "e4m3") @ mxq(f64(w_o), 1, "e4m3").T) + f64(b_o)

@@ -1,0 +1,231 @@
+from contextlib import ExitStack
+
+import concourse.mybir as mybir
+from concourse.masks import make_identity
+
+F32 = mybir.dt.float32
+BF16 = mybir.dt.bfloat16
+U32 = mybir.dt.uint32
+U8 = mybir.dt.uint8
+FP8X4 = mybir.dt.float8_e4m3fn_x4
+ACT = mybir.ActivationFunctionType
+ALU = mybir.AluOpType
+
+P = 128
+TOKENS = 2048
+FEAT = 1024
+OUTF = 1024
+EPS = 1e-8
+PACK = 4
+K_PASS = P * PACK
+PASSES = FEAT // K_PASS
+PAIR = 2
+WORD_COLS = FEAT // (PAIR * P)
+PLANES = FEAT // P
+BANK = 512
+GROUP_TILES = 4
+GROUP = GROUP_TILES * P
+GROUPS = TOKENS // GROUP
+OUT_HALVES = OUTF // BANK
+GPSIMD_TOKENS = 256
+
+FLOPS = 2 * TOKENS * FEAT * OUTF
+
+
+def tile_normlocalattention_pb_kernel(tc, attn_out, norm_scale, norm_gate, w_o, b_o, out):
+    nc = tc.nc
+    x_rows = attn_out.rearrange("l n e -> (l n) e")
+    out_rows = out.rearrange("l n f -> (l n) f")
+
+    with ExitStack() as stack:
+        keep = stack.enter_context(tc.tile_pool(name="keep", bufs=1))
+        planes = stack.enter_context(tc.tile_pool(name="planes", bufs=2))
+        small = stack.enter_context(tc.tile_pool(name="small", bufs=2))
+        scratch = stack.enter_context(tc.tile_pool(name="scratch", bufs=4))
+        results = stack.enter_context(tc.tile_pool(name="results", bufs=4))
+        flipped = stack.enter_context(tc.psum_pool(name="flipped", bufs=3))
+        spread = stack.enter_context(tc.psum_pool(name="spread", bufs=1))
+        sums = stack.enter_context(tc.psum_pool(name="sums", bufs=4))
+
+        ident = keep.tile([P, P], F32)
+        make_identity(nc, ident[:])
+        ones = keep.tile([P, P], BF16)
+        nc.vector.memset(ones[:], 1.0)
+        halves_exp = keep.tile([P, GROUP_TILES], F32)
+        nc.vector.memset(halves_exp[:], 0.5)
+        gains = keep.tile([P, PAIR * P], BF16)
+        nc.vector.memset(gains[:], 0.0)
+        bias_row = keep.tile([P, OUTF], BF16)
+        nc.vector.memset(bias_row[:], 0.0)
+
+        nc.scalar.dma_start(out=gains[0:WORD_COLS, :], in_=norm_gate.rearrange("(r c) -> r c", r=WORD_COLS))
+        nc.scalar.dma_start(
+            out=gains[WORD_COLS : 2 * WORD_COLS, :], in_=norm_scale.rearrange("(r c) -> r c", r=WORD_COLS)
+        )
+        nc.scalar.dma_start(out=bias_row[0:1, :], in_=b_o.rearrange("(r c) -> r c", r=1))
+
+        x_tiles = [keep.tile([P, FEAT], BF16, name="x%d" % i) for i in range(TOKENS // P)]
+        w_tiles = [keep.tile([P, FEAT], BF16, name="w%d" % i) for i in range(OUTF // P)]
+
+        def load_x(i):
+            nc.sync.dma_start(out=x_tiles[i][:], in_=x_rows[i * P : (i + 1) * P, :])
+
+        for i in range(GROUP_TILES):
+            load_x(i)
+        for i in range(OUTF // P):
+            nc.sync.dma_start(out=w_tiles[i][:], in_=w_o[i * P : (i + 1) * P, :])
+        for i in range(GROUP_TILES, TOKENS // P):
+            load_x(i)
+
+        gains_t = flipped.tile([P, P], F32, tag="flip")
+        nc.tensor.transpose(gains_t[:], gains[:].bitcast(F32), ident[:])
+        gain_cols = keep.tile([P, 2 * PLANES], F32)
+        nc.vector.tensor_copy(out=gain_cols[:], in_=gains_t[:].bitcast(BF16)[:, 0 : 2 * PLANES])
+
+        def gate_col(c):
+            return gain_cols[:, c : c + 1]
+
+        def scale_col(c):
+            return gain_cols[:, PLANES + c : PLANES + c + 1]
+
+        bias = keep.tile([P, OUTF], F32)
+        for h in range(OUT_HALVES):
+            cols = slice(h * BANK, (h + 1) * BANK)
+            bias_ps = sums.tile([P, BANK], F32, tag="sum")
+            nc.tensor.matmul(out=bias_ps[:], lhsT=ones[:], rhs=bias_row[:, cols], start=True, stop=True)
+            nc.vector.tensor_copy(out=bias[:, cols], in_=bias_ps[:])
+
+        w_codes = keep.tile([P, PASSES, OUTF], U32, align_bytes=64)
+        w_scales = keep.tile([P, PASSES, OUTF], U8, align_bytes=64)
+
+        def prepare_w():
+            for g in range(PASSES):
+                w_grouped = keep.tile([P, OUTF * PACK], BF16, name="w_grouped%d" % g, align_bytes=64)
+                w_words = w_grouped[:].bitcast(F32).rearrange("p (f u) -> p f u", u=PAIR)
+                for fp in range(OUTF // (2 * P)):
+                    w_t = flipped.tile([P, PAIR, 2 * P], F32, tag="flip")
+                    for u in range(PAIR):
+                        word_cols = slice((PAIR * g + u) * P, (PAIR * g + u + 1) * P)
+                        for o in range(2):
+                            nc.tensor.transpose(
+                                w_t[:, u, o * P : (o + 1) * P],
+                                w_tiles[2 * fp + o][:].bitcast(F32)[:, word_cols],
+                                ident[:],
+                            )
+                    nc.vector.tensor_copy(
+                        out=w_words[:, fp * 2 * P : (fp + 1) * 2 * P, :], in_=w_t[:].rearrange("p u f -> p f u")
+                    )
+                for h in range(OUT_HALVES):
+                    cols = slice(h * BANK, (h + 1) * BANK)
+                    nc.vector.quantize_mx(
+                        out=w_codes[:, g, cols].bitcast(FP8X4),
+                        scales=w_scales[:, g, cols],
+                        in_=w_grouped[:, h * BANK * PACK : (h + 1) * BANK * PACK],
+                    )
+
+        def gate_group(i):
+            sig = planes.tile([P, PLANES, GROUP], F32, name="sig")
+            z = planes.tile([P, PLANES, GROUP], F32, name="z")
+            for wc in range(WORD_COLS):
+                x_t = flipped.tile([P, GROUP], F32, tag="flip")
+                for j in range(GROUP_TILES):
+                    nc.tensor.transpose(
+                        x_t[:, j * P : (j + 1) * P],
+                        x_tiles[i * GROUP_TILES + j][:].bitcast(F32)[:, wc * P : (wc + 1) * P],
+                        ident[:],
+                    )
+                halves = x_t[:].bitcast(BF16).rearrange("p (k e) -> p k e", e=PAIR)
+                for e in range(PAIR):
+                    c = PAIR * wc + e
+                    nc.scalar.activation(out=sig[:, c, :], in_=halves[:, :, e], func=ACT.Sigmoid, scale=gate_col(c))
+                for e in range(PAIR):
+                    c = PAIR * wc + e
+                    nc.vector.scalar_tensor_tensor(
+                        out=z[:, c, :],
+                        in0=halves[:, :, e],
+                        scalar=scale_col(c),
+                        in1=sig[:, c, :],
+                        op0=ALU.mult,
+                        op1=ALU.mult,
+                    )
+            return z
+
+        def inverse_rms(i):
+            mean_sq = small.tile([P, GROUP_TILES], F32, name="mean_sq")
+            for j in range(GROUP_TILES):
+                squares = scratch.tile([P, FEAT], BF16, name="squares")
+                nc.scalar.activation(
+                    out=squares[:],
+                    in_=x_tiles[i * GROUP_TILES + j][:],
+                    func=ACT.Square,
+                    scale=1.0 / 32.0,
+                    accum_out=mean_sq[:, j : j + 1],
+                )
+            rms = small.tile([P, GROUP_TILES], F32, name="rms")
+            nc.gpsimd.tensor_tensor(out=rms[:], in0=mean_sq[:], in1=halves_exp[:], op=ALU.pow)
+            rms_eps = small.tile([P, GROUP_TILES], F32, name="rms_eps")
+            nc.vector.tensor_scalar_add(out=rms_eps[:], in0=rms[:], scalar1=EPS)
+            inv = small.tile([P, GROUP_TILES], F32, name="inv")
+            nc.vector.reciprocal(out=inv[:], in_=rms_eps[:])
+            inv_ps = spread.tile([P, GROUP], F32, name="inv_ps")
+            for j in range(GROUP_TILES):
+                nc.tensor.matmul(
+                    out=inv_ps[:, j * P : (j + 1) * P],
+                    lhsT=inv[:, j : j + 1].to_broadcast([P, P]),
+                    rhs=ident[:],
+                    start=True,
+                    stop=True,
+                )
+            inv_row = small.tile([P, GROUP], F32, name="inv_row")
+            nc.scalar.copy(out=inv_row[:], in_=inv_ps[:])
+            return inv_row
+
+        def finish_group(i, z, inv_row):
+            y_codes = small.tile([P, PASSES, GROUP], U32, name="y_codes", align_bytes=64)
+            y_scales = small.tile([P, PASSES, GROUP], U8, name="y_scales", align_bytes=64)
+            for g in range(PASSES):
+                y_grouped = small.tile([P, GROUP, PACK], BF16, name="y_grouped", align_bytes=64)
+                for engine, first, n in (
+                    (nc.gpsimd, 0, GPSIMD_TOKENS),
+                    (nc.vector, GPSIMD_TOKENS, GROUP - GPSIMD_TOKENS),
+                ):
+                    toks = slice(first, first + n)
+                    engine.tensor_tensor(
+                        out=y_grouped[:, toks, :],
+                        in0=z[:, g * PACK : (g + 1) * PACK, toks].rearrange("p t k -> p k t"),
+                        in1=inv_row[:, toks].unsqueeze(2).to_broadcast([P, n, PACK]),
+                        op=ALU.mult,
+                    )
+                nc.vector.quantize_mx(
+                    out=y_codes[:, g, :].bitcast(FP8X4),
+                    scales=y_scales[:, g, :],
+                    in_=y_grouped[:].rearrange("p k t -> p (k t)"),
+                )
+            for j in range(GROUP_TILES):
+                toks = slice(j * P, (j + 1) * P)
+                res = results.tile([P, OUTF], F32, name="res")
+                for h in range(OUT_HALVES):
+                    cols = slice(h * BANK, (h + 1) * BANK)
+                    acc = sums.tile([P, BANK], F32, tag="sum")
+                    for g in range(PASSES):
+                        nc.tensor.matmul_mx(
+                            out=acc[:],
+                            lhsT=y_codes[:, g, toks].bitcast(FP8X4),
+                            lhsT_scale=y_scales[:, g, toks],
+                            rhs=w_codes[:, g, cols].bitcast(FP8X4),
+                            rhs_scale=w_scales[:, g, cols],
+                            start=(g == 0),
+                            stop=(g == PASSES - 1),
+                        )
+                    nc.vector.tensor_tensor(out=res[:, cols], in0=acc[:], in1=bias[:, cols], op=ALU.add)
+                row0 = (i * GROUP_TILES + j) * P
+                nc.sync.dma_start(out=out_rows[row0 : row0 + P, :], in_=res[:])
+
+        ready = {}
+        for i in range(GROUPS + 1):
+            if i < GROUPS:
+                ready[i] = (gate_group(i), inverse_rms(i))
+            if i == 0:
+                prepare_w()
+            else:
+                finish_group(i - 1, ready[i - 1][0], ready[i - 1][1])

@@ -27,7 +27,6 @@ GROUP_TILES = 4
 GROUP = GROUP_TILES * P
 GROUPS = TOKENS // GROUP
 OUT_HALVES = OUTF // BANK
-GPSIMD_TOKENS = 256
 
 FLOPS = 2 * TOKENS * FEAT * OUTF
 
@@ -185,15 +184,12 @@ def tile_normlocalattention_pb_kernel(tc, attn_out, norm_scale, norm_gate, w_o, 
             y_scales = small.tile([P, PASSES, GROUP], U8, name="y_scales", align_bytes=64)
             for g in range(PASSES):
                 y_grouped = small.tile([P, GROUP, PACK], BF16, name="y_grouped", align_bytes=64)
-                for engine, first, n in (
-                    (nc.gpsimd, 0, GPSIMD_TOKENS),
-                    (nc.vector, GPSIMD_TOKENS, GROUP - GPSIMD_TOKENS),
-                ):
-                    toks = slice(first, first + n)
-                    engine.tensor_tensor(
+                for j in range(GROUP_TILES):
+                    toks = slice(j * P, (j + 1) * P)
+                    nc.gpsimd.tensor_tensor(
                         out=y_grouped[:, toks, :],
                         in0=z[:, g * PACK : (g + 1) * PACK, toks].rearrange("p t k -> p k t"),
-                        in1=inv_row[:, toks].unsqueeze(2).to_broadcast([P, n, PACK]),
+                        in1=inv_row[:, toks].unsqueeze(2).to_broadcast([P, P, PACK]),
                         op=ALU.mult,
                     )
                 nc.vector.quantize_mx(

@@ -27,6 +27,7 @@ GROUP_TILES = 4
 GROUP = GROUP_TILES * P
 GROUPS = TOKENS // GROUP
 OUT_HALVES = OUTF // BANK
+RUN = 4
 
 FLOPS = 2 * TOKENS * FEAT * OUTF
 
@@ -38,20 +39,21 @@ def tile_normlocalattention_pb_kernel(tc, attn_out, norm_scale, norm_gate, w_o, 
 
     with ExitStack() as stack:
         keep = stack.enter_context(tc.tile_pool(name="keep", bufs=1))
-        planes = stack.enter_context(tc.tile_pool(name="planes", bufs=2))
-        small = stack.enter_context(tc.tile_pool(name="small", bufs=2))
-        scratch = stack.enter_context(tc.tile_pool(name="scratch", bufs=4))
+        work = stack.enter_context(tc.tile_pool(name="work", bufs=2))
+        stats = stack.enter_context(tc.tile_pool(name="stats", bufs=4))
+        normed = stack.enter_context(tc.tile_pool(name="normed", bufs=2 * GROUP_TILES))
         results = stack.enter_context(tc.tile_pool(name="results", bufs=4))
-        flipped = stack.enter_context(tc.psum_pool(name="flipped", bufs=3))
-        spread = stack.enter_context(tc.psum_pool(name="spread", bufs=1))
-        sums = stack.enter_context(tc.psum_pool(name="sums", bufs=4))
+        flipped_x = stack.enter_context(tc.psum_pool(name="flipped_x", bufs=2))
+        flipped_n = stack.enter_context(tc.psum_pool(name="flipped_n", bufs=3))
+        sums = stack.enter_context(tc.psum_pool(name="sums", bufs=3))
 
         ident = keep.tile([P, P], F32)
         make_identity(nc, ident[:])
         ones = keep.tile([P, P], BF16)
         nc.vector.memset(ones[:], 1.0)
-        halves_exp = keep.tile([P, GROUP_TILES], F32)
-        nc.vector.memset(halves_exp[:], 0.5)
+        exponents = keep.tile([P, 2], F32)
+        nc.vector.memset(exponents[:, 0:1], 0.5)
+        nc.vector.memset(exponents[:, 1:2], -1.0)
         gains = keep.tile([P, PAIR * P], BF16)
         nc.vector.memset(gains[:], 0.0)
         bias_row = keep.tile([P, OUTF], BF16)
@@ -76,7 +78,7 @@ def tile_normlocalattention_pb_kernel(tc, attn_out, norm_scale, norm_gate, w_o, 
         for i in range(GROUP_TILES, TOKENS // P):
             load_x(i)
 
-        gains_t = flipped.tile([P, P], F32, tag="flip")
+        gains_t = flipped_x.tile([P, P], F32, tag="flip_x")
         nc.tensor.transpose(gains_t[:], gains[:].bitcast(F32), ident[:])
         gain_cols = keep.tile([P, 2 * PLANES], F32)
         nc.vector.tensor_copy(out=gain_cols[:], in_=gains_t[:].bitcast(BF16)[:, 0 : 2 * PLANES])
@@ -102,7 +104,7 @@ def tile_normlocalattention_pb_kernel(tc, attn_out, norm_scale, norm_gate, w_o, 
                 w_grouped = keep.tile([P, OUTF * PACK], BF16, name="w_grouped%d" % g, align_bytes=64)
                 w_words = w_grouped[:].bitcast(F32).rearrange("p (f u) -> p f u", u=PAIR)
                 for fp in range(OUTF // (2 * P)):
-                    w_t = flipped.tile([P, PAIR, 2 * P], F32, tag="flip")
+                    w_t = flipped_n.tile([P, PAIR, 2 * P], F32, tag="flip_n")
                     for u in range(PAIR):
                         word_cols = slice((PAIR * g + u) * P, (PAIR * g + u + 1) * P)
                         for o in range(2):
@@ -122,81 +124,76 @@ def tile_normlocalattention_pb_kernel(tc, attn_out, norm_scale, norm_gate, w_o, 
                         in_=w_grouped[:, h * BANK * PACK : (h + 1) * BANK * PACK],
                     )
 
-        def gate_group(i):
-            sig = planes.tile([P, PLANES, GROUP], F32, name="sig")
-            z = planes.tile([P, PLANES, GROUP], F32, name="z")
-            for wc in range(WORD_COLS):
-                x_t = flipped.tile([P, GROUP], F32, tag="flip")
-                for j in range(GROUP_TILES):
-                    nc.tensor.transpose(
-                        x_t[:, j * P : (j + 1) * P],
-                        x_tiles[i * GROUP_TILES + j][:].bitcast(F32)[:, wc * P : (wc + 1) * P],
-                        ident[:],
-                    )
-                halves = x_t[:].bitcast(BF16).rearrange("p (k e) -> p k e", e=PAIR)
-                for e in range(PAIR):
-                    c = PAIR * wc + e
-                    nc.scalar.activation(out=sig[:, c, :], in_=halves[:, :, e], func=ACT.Sigmoid, scale=gate_col(c))
-                for e in range(PAIR):
-                    c = PAIR * wc + e
+        def normalise(i):
+            mean_sq = stats.tile([P, 1], F32, name="mean_sq")
+            squares = stats.tile([P, FEAT], BF16, name="squares")
+            nc.scalar.activation(
+                out=squares[:], in_=x_tiles[i][:], func=ACT.Square, scale=1.0 / 32.0, accum_out=mean_sq[:]
+            )
+            rms = stats.tile([P, 1], F32, name="rms")
+            nc.gpsimd.tensor_tensor(out=rms[:], in0=mean_sq[:], in1=exponents[:, 0:1], op=ALU.pow)
+            rms_eps = stats.tile([P, 1], F32, name="rms_eps")
+            nc.gpsimd.tensor_scalar_add(out=rms_eps[:], in0=rms[:], scalar1=EPS)
+            inv = stats.tile([P, 1], F32, name="inv")
+            nc.gpsimd.tensor_tensor(out=inv[:], in0=rms_eps[:], in1=exponents[:, 1:2], op=ALU.pow)
+            x_n = normed.tile([P, FEAT], F32, name="x_n")
+            nc.gpsimd.tensor_scalar(
+                out=x_n[:].rearrange("p (w e q) -> p w e q", e=PAIR, q=P),
+                in0=x_tiles[i][:].rearrange("p (w q e) -> p w e q", e=PAIR, q=P),
+                scalar1=inv[:],
+                scalar2=0.0,
+                op0=ALU.mult,
+                op1=ALU.add,
+            )
+            return x_n
+
+        def gate_group(i, x_n):
+            y_codes = work.tile([P, PASSES, GROUP], U32, name="y_codes", align_bytes=64)
+            y_scales = work.tile([P, PASSES, GROUP], U8, name="y_scales", align_bytes=64)
+            for g in range(PASSES):
+                sig = work.tile([P, PACK, GROUP], F32, name="sig")
+                y_planes = work.tile([P, PACK, GROUP], BF16, name="y_planes")
+                for u in range(PAIR):
+                    wc = PAIR * g + u
+                    x_t = flipped_x.tile([P, GROUP], F32, tag="flip_x")
+                    for j in range(GROUP_TILES):
+                        nc.tensor.transpose(
+                            x_t[:, j * P : (j + 1) * P],
+                            x_tiles[i * GROUP_TILES + j][:].bitcast(F32)[:, wc * P : (wc + 1) * P],
+                            ident[:],
+                        )
+                    halves = x_t[:].bitcast(BF16).rearrange("p (k e) -> p k e", e=PAIR)
+                    for e in range(PAIR):
+                        t = PAIR * u + e
+                        nc.scalar.activation(
+                            out=sig[:, t, :], in_=halves[:, :, e], func=ACT.Sigmoid, scale=gate_col(PACK * g + t)
+                        )
+                for t in range(PACK):
+                    c = PACK * g + t
+                    n_t = flipped_n.tile([P, GROUP], F32, tag="flip_n")
+                    for j in range(GROUP_TILES):
+                        nc.tensor.transpose(n_t[:, j * P : (j + 1) * P], x_n[j][:, c * P : (c + 1) * P], ident[:])
                     nc.vector.scalar_tensor_tensor(
-                        out=z[:, c, :],
-                        in0=halves[:, :, e],
+                        out=y_planes[:, t, :],
+                        in0=n_t[:],
                         scalar=scale_col(c),
-                        in1=sig[:, c, :],
+                        in1=sig[:, t, :],
                         op0=ALU.mult,
                         op1=ALU.mult,
                     )
-            return z
-
-        def inverse_rms(i):
-            mean_sq = small.tile([P, GROUP_TILES], F32, name="mean_sq")
-            for j in range(GROUP_TILES):
-                squares = scratch.tile([P, FEAT], BF16, name="squares")
-                nc.scalar.activation(
-                    out=squares[:],
-                    in_=x_tiles[i * GROUP_TILES + j][:],
-                    func=ACT.Square,
-                    scale=1.0 / 32.0,
-                    accum_out=mean_sq[:, j : j + 1],
+                y_grouped = work.tile([P, GROUP, PACK], BF16, name="y_grouped", align_bytes=64)
+                nc.vector.tensor_copy(
+                    out=y_grouped[:].rearrange("p (c i) t -> p c t i", i=RUN),
+                    in_=y_planes[:].rearrange("p t (c i) -> p c t i", i=RUN),
                 )
-            rms = small.tile([P, GROUP_TILES], F32, name="rms")
-            nc.gpsimd.tensor_tensor(out=rms[:], in0=mean_sq[:], in1=halves_exp[:], op=ALU.pow)
-            rms_eps = small.tile([P, GROUP_TILES], F32, name="rms_eps")
-            nc.vector.tensor_scalar_add(out=rms_eps[:], in0=rms[:], scalar1=EPS)
-            inv = small.tile([P, GROUP_TILES], F32, name="inv")
-            nc.vector.reciprocal(out=inv[:], in_=rms_eps[:])
-            inv_ps = spread.tile([P, GROUP], F32, name="inv_ps")
-            for j in range(GROUP_TILES):
-                nc.tensor.matmul(
-                    out=inv_ps[:, j * P : (j + 1) * P],
-                    lhsT=inv[:, j : j + 1].to_broadcast([P, P]),
-                    rhs=ident[:],
-                    start=True,
-                    stop=True,
-                )
-            inv_row = small.tile([P, GROUP], F32, name="inv_row")
-            nc.scalar.copy(out=inv_row[:], in_=inv_ps[:])
-            return inv_row
-
-        def finish_group(i, z, inv_row):
-            y_codes = small.tile([P, PASSES, GROUP], U32, name="y_codes", align_bytes=64)
-            y_scales = small.tile([P, PASSES, GROUP], U8, name="y_scales", align_bytes=64)
-            for g in range(PASSES):
-                y_grouped = small.tile([P, GROUP, PACK], BF16, name="y_grouped", align_bytes=64)
-                for j in range(GROUP_TILES):
-                    toks = slice(j * P, (j + 1) * P)
-                    nc.gpsimd.tensor_tensor(
-                        out=y_grouped[:, toks, :],
-                        in0=z[:, g * PACK : (g + 1) * PACK, toks].rearrange("p t k -> p k t"),
-                        in1=inv_row[:, toks].unsqueeze(2).to_broadcast([P, P, PACK]),
-                        op=ALU.mult,
-                    )
                 nc.vector.quantize_mx(
                     out=y_codes[:, g, :].bitcast(FP8X4),
                     scales=y_scales[:, g, :],
                     in_=y_grouped[:].rearrange("p k t -> p (k t)"),
                 )
+            return y_codes, y_scales
+
+        def multiply_group(i, y_codes, y_scales):
             for j in range(GROUP_TILES):
                 toks = slice(j * P, (j + 1) * P)
                 res = results.tile([P, OUTF], F32, name="res")
@@ -217,11 +214,12 @@ def tile_normlocalattention_pb_kernel(tc, attn_out, norm_scale, norm_gate, w_o, 
                 row0 = (i * GROUP_TILES + j) * P
                 nc.sync.dma_start(out=out_rows[row0 : row0 + P, :], in_=res[:])
 
-        ready = {}
+        quantised = {}
         for i in range(GROUPS + 1):
             if i < GROUPS:
-                ready[i] = (gate_group(i), inverse_rms(i))
+                x_n = [normalise(i * GROUP_TILES + j) for j in range(GROUP_TILES)]
+                quantised[i] = gate_group(i, x_n)
             if i == 0:
                 prepare_w()
             else:
-                finish_group(i - 1, ready[i - 1][0], ready[i - 1][1])
+                multiply_group(i - 1, quantised[i - 1][0], quantised[i - 1][1])

@@ -27,7 +27,6 @@ GROUP_TILES = 4
 GROUP = GROUP_TILES * P
 GROUPS = TOKENS // GROUP
 OUT_HALVES = OUTF // BANK
-RUN = 4
 
 FLOPS = 2 * TOKENS * FEAT * OUTF
 
@@ -39,21 +38,20 @@ def tile_normlocalattention_pb_kernel(tc, attn_out, norm_scale, norm_gate, w_o, 
 
     with ExitStack() as stack:
         keep = stack.enter_context(tc.tile_pool(name="keep", bufs=1))
-        work = stack.enter_context(tc.tile_pool(name="work", bufs=2))
-        stats = stack.enter_context(tc.tile_pool(name="stats", bufs=4))
-        normed = stack.enter_context(tc.tile_pool(name="normed", bufs=2 * GROUP_TILES))
+        planes = stack.enter_context(tc.tile_pool(name="planes", bufs=2))
+        small = stack.enter_context(tc.tile_pool(name="small", bufs=2))
+        scratch = stack.enter_context(tc.tile_pool(name="scratch", bufs=4))
         results = stack.enter_context(tc.tile_pool(name="results", bufs=4))
-        flipped_x = stack.enter_context(tc.psum_pool(name="flipped_x", bufs=2))
-        flipped_n = stack.enter_context(tc.psum_pool(name="flipped_n", bufs=3))
+        flipped = stack.enter_context(tc.psum_pool(name="flipped", bufs=3))
+        spread = stack.enter_context(tc.psum_pool(name="spread", bufs=2))
         sums = stack.enter_context(tc.psum_pool(name="sums", bufs=3))
 
         ident = keep.tile([P, P], F32)
         make_identity(nc, ident[:])
         ones = keep.tile([P, P], BF16)
         nc.vector.memset(ones[:], 1.0)
-        exponents = keep.tile([P, 2], F32)
-        nc.vector.memset(exponents[:, 0:1], 0.5)
-        nc.vector.memset(exponents[:, 1:2], -1.0)
+        halves_exp = keep.tile([P, GROUP_TILES], F32)
+        nc.vector.memset(halves_exp[:], 0.5)
         gains = keep.tile([P, PAIR * P], BF16)
         nc.vector.memset(gains[:], 0.0)
         bias_row = keep.tile([P, OUTF], BF16)
@@ -78,7 +76,7 @@ def tile_normlocalattention_pb_kernel(tc, attn_out, norm_scale, norm_gate, w_o, 
         for i in range(GROUP_TILES, TOKENS // P):
             load_x(i)
 
-        gains_t = flipped_x.tile([P, P], F32, tag="flip_x")
+        gains_t = flipped.tile([P, P], F32, tag="flip")
         nc.tensor.transpose(gains_t[:], gains[:].bitcast(F32), ident[:])
         gain_cols = keep.tile([P, 2 * PLANES], F32)
         nc.vector.tensor_copy(out=gain_cols[:], in_=gains_t[:].bitcast(BF16)[:, 0 : 2 * PLANES])
@@ -104,7 +102,7 @@ def tile_normlocalattention_pb_kernel(tc, attn_out, norm_scale, norm_gate, w_o, 
                 w_grouped = keep.tile([P, OUTF * PACK], BF16, name="w_grouped%d" % g, align_bytes=64)
                 w_words = w_grouped[:].bitcast(F32).rearrange("p (f u) -> p f u", u=PAIR)
                 for fp in range(OUTF // (2 * P)):
-                    w_t = flipped_n.tile([P, PAIR, 2 * P], F32, tag="flip_n")
+                    w_t = flipped.tile([P, PAIR, 2 * P], F32, tag="flip")
                     for u in range(PAIR):
                         word_cols = slice((PAIR * g + u) * P, (PAIR * g + u + 1) * P)
                         for o in range(2):
@@ -124,76 +122,77 @@ def tile_normlocalattention_pb_kernel(tc, attn_out, norm_scale, norm_gate, w_o, 
                         in_=w_grouped[:, h * BANK * PACK : (h + 1) * BANK * PACK],
                     )
 
-        def normalise(i):
-            mean_sq = stats.tile([P, 1], F32, name="mean_sq")
-            squares = stats.tile([P, FEAT], BF16, name="squares")
-            nc.scalar.activation(
-                out=squares[:], in_=x_tiles[i][:], func=ACT.Square, scale=1.0 / 32.0, accum_out=mean_sq[:]
-            )
-            rms = stats.tile([P, 1], F32, name="rms")
-            nc.gpsimd.tensor_tensor(out=rms[:], in0=mean_sq[:], in1=exponents[:, 0:1], op=ALU.pow)
-            rms_eps = stats.tile([P, 1], F32, name="rms_eps")
-            nc.gpsimd.tensor_scalar_add(out=rms_eps[:], in0=rms[:], scalar1=EPS)
-            inv = stats.tile([P, 1], F32, name="inv")
-            nc.gpsimd.tensor_tensor(out=inv[:], in0=rms_eps[:], in1=exponents[:, 1:2], op=ALU.pow)
-            x_n = normed.tile([P, FEAT], F32, name="x_n")
-            nc.gpsimd.tensor_scalar(
-                out=x_n[:].rearrange("p (w e q) -> p w e q", e=PAIR, q=P),
-                in0=x_tiles[i][:].rearrange("p (w q e) -> p w e q", e=PAIR, q=P),
-                scalar1=inv[:],
-                scalar2=0.0,
-                op0=ALU.mult,
-                op1=ALU.add,
-            )
-            return x_n
-
-        def gate_group(i, x_n):
-            y_codes = work.tile([P, PASSES, GROUP], U32, name="y_codes", align_bytes=64)
-            y_scales = work.tile([P, PASSES, GROUP], U8, name="y_scales", align_bytes=64)
-            for g in range(PASSES):
-                sig = work.tile([P, PACK, GROUP], F32, name="sig")
-                y_planes = work.tile([P, PACK, GROUP], BF16, name="y_planes")
-                for u in range(PAIR):
-                    wc = PAIR * g + u
-                    x_t = flipped_x.tile([P, GROUP], F32, tag="flip_x")
-                    for j in range(GROUP_TILES):
-                        nc.tensor.transpose(
-                            x_t[:, j * P : (j + 1) * P],
-                            x_tiles[i * GROUP_TILES + j][:].bitcast(F32)[:, wc * P : (wc + 1) * P],
-                            ident[:],
-                        )
-                    halves = x_t[:].bitcast(BF16).rearrange("p (k e) -> p k e", e=PAIR)
-                    for e in range(PAIR):
-                        t = PAIR * u + e
-                        nc.scalar.activation(
-                            out=sig[:, t, :], in_=halves[:, :, e], func=ACT.Sigmoid, scale=gate_col(PACK * g + t)
-                        )
-                for t in range(PACK):
-                    c = PACK * g + t
-                    n_t = flipped_n.tile([P, GROUP], F32, tag="flip_n")
-                    for j in range(GROUP_TILES):
-                        nc.tensor.transpose(n_t[:, j * P : (j + 1) * P], x_n[j][:, c * P : (c + 1) * P], ident[:])
+        def gate_group(i):
+            sig = planes.tile([P, PLANES, GROUP], F32, name="sig")
+            z = planes.tile([P, PLANES, GROUP], F32, name="z")
+            for wc in range(WORD_COLS):
+                x_t = flipped.tile([P, GROUP], F32, tag="flip")
+                for j in range(GROUP_TILES):
+                    nc.tensor.transpose(
+                        x_t[:, j * P : (j + 1) * P],
+                        x_tiles[i * GROUP_TILES + j][:].bitcast(F32)[:, wc * P : (wc + 1) * P],
+                        ident[:],
+                    )
+                halves = x_t[:].bitcast(BF16).rearrange("p (k e) -> p k e", e=PAIR)
+                for e in range(PAIR):
+                    c = PAIR * wc + e
+                    nc.scalar.activation(out=sig[:, c, :], in_=halves[:, :, e], func=ACT.Sigmoid, scale=gate_col(c))
+                for e in range(PAIR):
+                    c = PAIR * wc + e
                     nc.vector.scalar_tensor_tensor(
-                        out=y_planes[:, t, :],
-                        in0=n_t[:],
+                        out=z[:, c, :],
+                        in0=halves[:, :, e],
                         scalar=scale_col(c),
-                        in1=sig[:, t, :],
+                        in1=sig[:, c, :],
                         op0=ALU.mult,
                         op1=ALU.mult,
                     )
-                y_grouped = work.tile([P, GROUP, PACK], BF16, name="y_grouped", align_bytes=64)
-                nc.vector.tensor_copy(
-                    out=y_grouped[:].rearrange("p (c i) t -> p c t i", i=RUN),
-                    in_=y_planes[:].rearrange("p t (c i) -> p c t i", i=RUN),
+            return z
+
+        def inverse_rms(i):
+            mean_sq = small.tile([P, GROUP_TILES], F32, name="mean_sq")
+            for j in range(GROUP_TILES):
+                squares = scratch.tile([P, FEAT], BF16, name="squares")
+                nc.scalar.activation(
+                    out=squares[:],
+                    in_=x_tiles[i * GROUP_TILES + j][:],
+                    func=ACT.Square,
+                    scale=1.0 / 32.0,
+                    accum_out=mean_sq[:, j : j + 1],
+                )
+            rms = small.tile([P, GROUP_TILES], F32, name="rms")
+            nc.gpsimd.tensor_tensor(out=rms[:], in0=mean_sq[:], in1=halves_exp[:], op=ALU.pow)
+            rms_eps = small.tile([P, GROUP_TILES], F32, name="rms_eps")
+            nc.vector.tensor_scalar_add(out=rms_eps[:], in0=rms[:], scalar1=EPS)
+            inv = small.tile([P, GROUP_TILES], F32, name="inv")
+            nc.vector.reciprocal(out=inv[:], in_=rms_eps[:])
+            inv_ps = spread.tile([P, GROUP], F32, name="inv_ps")
+            for j in range(GROUP_TILES):
+                nc.tensor.matmul(
+                    out=inv_ps[:, j * P : (j + 1) * P],
+                    lhsT=inv[:, j : j + 1].to_broadcast([P, P]),
+                    rhs=ident[:],
+                    start=True,
+                    stop=True,
+                )
+            return inv_ps
+
+        def finish_group(i, z, inv_row):
+            y_codes = small.tile([P, PASSES, GROUP], U32, name="y_codes", align_bytes=64)
+            y_scales = small.tile([P, PASSES, GROUP], U8, name="y_scales", align_bytes=64)
+            for g in range(PASSES):
+                y_grouped = small.tile([P, GROUP, PACK], BF16, name="y_grouped", align_bytes=64)
+                nc.vector.tensor_tensor(
+                    out=y_grouped[:],
+                    in0=z[:, g * PACK : (g + 1) * PACK, :].rearrange("p t k -> p k t"),
+                    in1=inv_row[:].unsqueeze(2).to_broadcast([P, GROUP, PACK]),
+                    op=ALU.mult,
                 )
                 nc.vector.quantize_mx(
                     out=y_codes[:, g, :].bitcast(FP8X4),
                     scales=y_scales[:, g, :],
                     in_=y_grouped[:].rearrange("p k t -> p (k t)"),
                 )
-            return y_codes, y_scales
-
-        def multiply_group(i, y_codes, y_scales):
             for j in range(GROUP_TILES):
                 toks = slice(j * P, (j + 1) * P)
                 res = results.tile([P, OUTF], F32, name="res")
@@ -214,12 +213,11 @@ def tile_normlocalattention_pb_kernel(tc, attn_out, norm_scale, norm_gate, w_o, 
                 row0 = (i * GROUP_TILES + j) * P
                 nc.sync.dma_start(out=out_rows[row0 : row0 + P, :], in_=res[:])
 
-        quantised = {}
+        ready = {}
         for i in range(GROUPS + 1):
             if i < GROUPS:
-                x_n = [normalise(i * GROUP_TILES + j) for j in range(GROUP_TILES)]
-                quantised[i] = gate_group(i, x_n)
+                ready[i] = (gate_group(i), inverse_rms(i))
             if i == 0:
                 prepare_w()
             else:
-                multiply_group(i - 1, quantised[i - 1][0], quantised[i - 1][1])
+                finish_group(i - 1, ready[i - 1][0], ready[i - 1][1])

from contextlib import ExitStack

import concourse.mybir as mybir
from concourse.masks import make_identity

F32 = mybir.dt.float32
BF16 = mybir.dt.bfloat16
U32 = mybir.dt.uint32
U8 = mybir.dt.uint8
FP8X4 = mybir.dt.float8_e4m3fn_x4
ACT = mybir.ActivationFunctionType
ALU = mybir.AluOpType

P = 128
TOKENS = 2048
FEAT = 1024
OUTF = 1024
EPS = 1e-8
PACK = 4
K_PASS = P * PACK
PASSES = FEAT // K_PASS
PAIR = 2
WORD_COLS = FEAT // (PAIR * P)
PLANES = FEAT // P
BANK = 512
GROUP_TILES = 4
GROUP = GROUP_TILES * P
GROUPS = TOKENS // GROUP
OUT_HALVES = OUTF // BANK

FLOPS = 2 * TOKENS * FEAT * OUTF


def tile_normlocalattention_pb_kernel(tc, attn_out, norm_scale, norm_gate, w_o, b_o, out):
    nc = tc.nc
    x_rows = attn_out.rearrange("l n e -> (l n) e")
    out_rows = out.rearrange("l n f -> (l n) f")

    with ExitStack() as stack:
        keep = stack.enter_context(tc.tile_pool(name="keep", bufs=1))
        planes = stack.enter_context(tc.tile_pool(name="planes", bufs=2))
        small = stack.enter_context(tc.tile_pool(name="small", bufs=2))
        scratch = stack.enter_context(tc.tile_pool(name="scratch", bufs=4))
        results = stack.enter_context(tc.tile_pool(name="results", bufs=4))
        flipped = stack.enter_context(tc.psum_pool(name="flipped", bufs=3))
        spread = stack.enter_context(tc.psum_pool(name="spread", bufs=2))
        sums = stack.enter_context(tc.psum_pool(name="sums", bufs=3))

        ident = keep.tile([P, P], F32)
        make_identity(nc, ident[:])
        ones = keep.tile([P, P], BF16)
        nc.vector.memset(ones[:], 1.0)
        halves_exp = keep.tile([P, GROUP_TILES], F32)
        nc.vector.memset(halves_exp[:], 0.5)
        gains = keep.tile([P, PAIR * P], BF16)
        nc.vector.memset(gains[:], 0.0)
        bias_row = keep.tile([P, OUTF], BF16)
        nc.vector.memset(bias_row[:], 0.0)

        nc.scalar.dma_start(out=gains[0:WORD_COLS, :], in_=norm_gate.rearrange("(r c) -> r c", r=WORD_COLS))
        nc.scalar.dma_start(
            out=gains[WORD_COLS : 2 * WORD_COLS, :], in_=norm_scale.rearrange("(r c) -> r c", r=WORD_COLS)
        )
        nc.scalar.dma_start(out=bias_row[0:1, :], in_=b_o.rearrange("(r c) -> r c", r=1))

        x_tiles = [keep.tile([P, FEAT], BF16, name="x%d" % i) for i in range(TOKENS // P)]
        w_tiles = [keep.tile([P, FEAT], BF16, name="w%d" % i) for i in range(OUTF // P)]

        def load_x(i):
            nc.sync.dma_start(out=x_tiles[i][:], in_=x_rows[i * P : (i + 1) * P, :])

        for i in range(GROUP_TILES):
            load_x(i)
        for i in range(OUTF // P):
            nc.sync.dma_start(out=w_tiles[i][:], in_=w_o[i * P : (i + 1) * P, :])
        for i in range(GROUP_TILES, TOKENS // P):
            load_x(i)

        gains_t = flipped.tile([P, P], F32, tag="flip")
        nc.tensor.transpose(gains_t[:], gains[:].bitcast(F32), ident[:])
        gain_cols = keep.tile([P, 2 * PLANES], F32)
        nc.vector.tensor_copy(out=gain_cols[:], in_=gains_t[:].bitcast(BF16)[:, 0 : 2 * PLANES])

        def gate_col(c):
            return gain_cols[:, c : c + 1]

        def scale_col(c):
            return gain_cols[:, PLANES + c : PLANES + c + 1]

        bias = keep.tile([P, OUTF], F32)
        for h in range(OUT_HALVES):
            cols = slice(h * BANK, (h + 1) * BANK)
            bias_ps = sums.tile([P, BANK], F32, tag="sum")
            nc.tensor.matmul(out=bias_ps[:], lhsT=ones[:], rhs=bias_row[:, cols], start=True, stop=True)
            nc.vector.tensor_copy(out=bias[:, cols], in_=bias_ps[:])

        w_codes = keep.tile([P, PASSES, OUTF], U32, align_bytes=64)
        w_scales = keep.tile([P, PASSES, OUTF], U8, align_bytes=64)

        def prepare_w():
            for g in range(PASSES):
                w_grouped = keep.tile([P, OUTF * PACK], BF16, name="w_grouped%d" % g, align_bytes=64)
                w_words = w_grouped[:].bitcast(F32).rearrange("p (f u) -> p f u", u=PAIR)
                for fp in range(OUTF // (2 * P)):
                    w_t = flipped.tile([P, PAIR, 2 * P], F32, tag="flip")
                    for u in range(PAIR):
                        word_cols = slice((PAIR * g + u) * P, (PAIR * g + u + 1) * P)
                        for o in range(2):
                            nc.tensor.transpose(
                                w_t[:, u, o * P : (o + 1) * P],
                                w_tiles[2 * fp + o][:].bitcast(F32)[:, word_cols],
                                ident[:],
                            )
                    nc.vector.tensor_copy(
                        out=w_words[:, fp * 2 * P : (fp + 1) * 2 * P, :], in_=w_t[:].rearrange("p u f -> p f u")
                    )
                for h in range(OUT_HALVES):
                    cols = slice(h * BANK, (h + 1) * BANK)
                    nc.vector.quantize_mx(
                        out=w_codes[:, g, cols].bitcast(FP8X4),
                        scales=w_scales[:, g, cols],
                        in_=w_grouped[:, h * BANK * PACK : (h + 1) * BANK * PACK],
                    )

        def gate_group(i):
            sig = planes.tile([P, PLANES, GROUP], F32, name="sig")
            z = planes.tile([P, PLANES, GROUP], F32, name="z")
            for wc in range(WORD_COLS):
                x_t = flipped.tile([P, GROUP], F32, tag="flip")
                for j in range(GROUP_TILES):
                    nc.tensor.transpose(
                        x_t[:, j * P : (j + 1) * P],
                        x_tiles[i * GROUP_TILES + j][:].bitcast(F32)[:, wc * P : (wc + 1) * P],
                        ident[:],
                    )
                halves = x_t[:].bitcast(BF16).rearrange("p (k e) -> p k e", e=PAIR)
                for e in range(PAIR):
                    c = PAIR * wc + e
                    nc.scalar.activation(out=sig[:, c, :], in_=halves[:, :, e], func=ACT.Sigmoid, scale=gate_col(c))
                for e in range(PAIR):
                    c = PAIR * wc + e
                    nc.vector.scalar_tensor_tensor(
                        out=z[:, c, :],
                        in0=halves[:, :, e],
                        scalar=scale_col(c),
                        in1=sig[:, c, :],
                        op0=ALU.mult,
                        op1=ALU.mult,
                    )
            return z

        def inverse_rms(i):
            mean_sq = small.tile([P, GROUP_TILES], F32, name="mean_sq")
            for j in range(GROUP_TILES):
                squares = scratch.tile([P, FEAT], BF16, name="squares")
                nc.scalar.activation(
                    out=squares[:],
                    in_=x_tiles[i * GROUP_TILES + j][:],
                    func=ACT.Square,
                    scale=1.0 / 32.0,
                    accum_out=mean_sq[:, j : j + 1],
                )
            rms = small.tile([P, GROUP_TILES], F32, name="rms")
            nc.gpsimd.tensor_tensor(out=rms[:], in0=mean_sq[:], in1=halves_exp[:], op=ALU.pow)
            rms_eps = small.tile([P, GROUP_TILES], F32, name="rms_eps")
            nc.vector.tensor_scalar_add(out=rms_eps[:], in0=rms[:], scalar1=EPS)
            inv = small.tile([P, GROUP_TILES], F32, name="inv")
            nc.vector.reciprocal(out=inv[:], in_=rms_eps[:])
            inv_ps = spread.tile([P, GROUP], F32, name="inv_ps")
            for j in range(GROUP_TILES):
                nc.tensor.matmul(
                    out=inv_ps[:, j * P : (j + 1) * P],
                    lhsT=inv[:, j : j + 1].to_broadcast([P, P]),
                    rhs=ident[:],
                    start=True,
                    stop=True,
                )
            return inv_ps

        def finish_group(i, z, inv_row):
            y_codes = small.tile([P, PASSES, GROUP], U32, name="y_codes", align_bytes=64)
            y_scales = small.tile([P, PASSES, GROUP], U8, name="y_scales", align_bytes=64)
            for g in range(PASSES):
                y_grouped = small.tile([P, GROUP, PACK], BF16, name="y_grouped", align_bytes=64)
                nc.vector.tensor_tensor(
                    out=y_grouped[:],
                    in0=z[:, g * PACK : (g + 1) * PACK, :].rearrange("p t k -> p k t"),
                    in1=inv_row[:].unsqueeze(2).to_broadcast([P, GROUP, PACK]),
                    op=ALU.mult,
                )
                nc.vector.quantize_mx(
                    out=y_codes[:, g, :].bitcast(FP8X4),
                    scales=y_scales[:, g, :],
                    in_=y_grouped[:].rearrange("p k t -> p (k t)"),
                )
            for j in range(GROUP_TILES):
                toks = slice(j * P, (j + 1) * P)
                res = results.tile([P, OUTF], F32, name="res")
                for h in range(OUT_HALVES):
                    cols = slice(h * BANK, (h + 1) * BANK)
                    acc = sums.tile([P, BANK], F32, tag="sum")
                    for g in range(PASSES):
                        nc.tensor.matmul_mx(
                            out=acc[:],
                            lhsT=y_codes[:, g, toks].bitcast(FP8X4),
                            lhsT_scale=y_scales[:, g, toks],
                            rhs=w_codes[:, g, cols].bitcast(FP8X4),
                            rhs_scale=w_scales[:, g, cols],
                            start=(g == 0),
                            stop=(g == PASSES - 1),
                        )
                    nc.vector.tensor_tensor(out=res[:, cols], in0=acc[:], in1=bias[:, cols], op=ALU.add)
                row0 = (i * GROUP_TILES + j) * P
                nc.sync.dma_start(out=out_rows[row0 : row0 + P, :], in_=res[:])

        ready = {}
        for i in range(GROUPS + 1):
            if i < GROUPS:
                ready[i] = (gate_group(i), inverse_rms(i))
            if i == 0:
                prepare_w()
            else:
                finish_group(i - 1, ready[i - 1][0], ready[i - 1][1])
